import numpy as np
import ml_dtypes

BF16 = ml_dtypes.bfloat16


def bf(x):
    return np.asarray(x, np.float32).astype(BF16)


def f32(x):
    return np.asarray(x, np.float32)


def f64(x):
    return np.asarray(x).astype(np.float64)


def striped(idx):
    return np.tile(idx.reshape(-1, 16).T, (8, 1))


CK, S, N, M, V = 128, 512, 128, 512, 256


def setup_inputs():
    return {
        "query_key": f32(np.random.standard_normal((CK, S))),
        "query_selection": f32(np.random.uniform(0.0, 1.0, (CK, N))),
        "memory_key": bf(np.random.standard_normal((CK, M))),
        "memory_shrinkage": f32(0.8 + 0.4 * np.random.uniform(0.0, 1.0, (M, 1))),
        "memory_value": bf(np.random.standard_normal((M, V))),
        "offs": striped(np.random.permutation(S)[:N]),
    }


def reference(query_key, query_selection, memory_key, memory_shrinkage, memory_value, offs):
    idx = offs[:16].T.reshape(-1)
    qe = f64(query_selection)
    mk = f64(memory_key)
    qs = f64(query_key)[:, idx] * qe
    b_sq = (f64(query_key)[:, idx] * qs).sum(axis=0, keepdims=True)
    keys = np.concatenate([2.0 * mk, -mk * mk], axis=0)
    quer = np.concatenate([qs, qe], axis=0)
    sim = (keys.T @ quer - b_sq) * f64(memory_shrinkage) / np.sqrt(CK)
    e = np.exp(sim)
    aff = e / e.sum(axis=0, keepdims=True)
    return f64(memory_value).T @ aff

@@ -1,0 +1,97 @@
+import math
+
+import concourse.mybir as mybir
+from concourse.masks import make_identity
+
+F32 = mybir.dt.float32
+BF16 = mybir.dt.bfloat16
+U16 = mybir.dt.uint16
+ALU = mybir.AluOpType
+FUNC = mybir.ActivationFunctionType
+
+P = 128
+CK, S, N, M, V = 128, 512, 128, 512, 256
+SLOT_BLOCKS = M // P
+VALUE_BLOCKS = V // P
+
+FLOPS = 2 * (2 * CK) * M * N + 2 * CK * N + 2 * M * V * N
+
+
+def tile_xmem_kernel(
+    tc, query_key, query_selection, memory_key, memory_shrinkage, memory_value, offs, out
+):
+    nc = tc.nc
+    with (
+        tc.tile_pool(name="held", bufs=1) as held,
+        tc.psum_pool(name="psum", bufs=1) as psum,
+    ):
+        offsets = held.tile([P, N // 16], U16, name="offsets")
+        nc.sync.dma_start(offsets[:], offs)
+        keys = held.tile([CK, S], F32, name="keys")
+        nc.sync.dma_start(keys[:], query_key)
+        sel = held.tile([CK, N], F32, name="sel")
+        nc.scalar.dma_start(sel[:], query_selection)
+        mk = held.tile([CK, M], BF16, name="mk")
+        nc.scalar.dma_start(mk[:], memory_key)
+        shrink = held.tile([P, M], F32, name="shrink")
+        nc.sync.dma_start(shrink[:], memory_shrinkage.rearrange("m o -> (m o)").partition_broadcast(P))
+        mv = held.tile([P, SLOT_BLOCKS, V], BF16, name="mv")
+        nc.scalar.dma_start(mv[:], memory_value.rearrange("(b p) v -> p b v", p=P))
+
+        ident = held.tile([P, P], BF16, name="ident")
+        make_identity(nc, ident[:])
+        ones = held.tile([CK, 1], F32, name="ones")
+        nc.vector.memset(ones[:], 1.0)
+
+        sel_k = held.tile([CK, N], F32, name="sel_k")
+        nc.vector.tensor_scalar_mul(sel_k[:], sel[:], 1.0 / math.sqrt(CK))
+        sel_bf = held.tile([CK, N], BF16, name="sel_bf")
+        nc.scalar.copy(sel_bf[:], sel_k[:])
+        mk_sq = held.tile([CK, M], BF16, name="mk_sq")
+        nc.vector.tensor_tensor(mk_sq[:], mk[:], mk[:], ALU.mult)
+
+        qs = held.tile([CK, N], F32, name="qs")
+        nc.vector.tensor_tensor(qs[:], keys[:].indirect(offsets[:]), sel_k[:], ALU.mult)
+        qqs = held.tile([CK, N], F32, name="qqs")
+        nc.vector.tensor_tensor(qqs[:], keys[:].indirect(offsets[:]), qs[:], ALU.mult)
+        qs_m2 = held.tile([CK, N], BF16, name="qs_m2")
+        nc.scalar.mul(qs_m2[:], qs[:], -2.0)
+
+        cross = psum.tile([N, M], F32, name="cross")
+        nc.tensor.matmul(cross[:], sel_bf[:], mk_sq[:], start=True, stop=False)
+        nc.tensor.matmul(cross[:], qs_m2[:], mk[:], start=False, stop=True)
+        b_sq = psum.tile([N, 1], F32, name="b_sq")
+        nc.tensor.matmul(b_sq[:], qqs[:], ones[:], start=True, stop=True)
+
+        dist = held.tile([N, M], F32, name="dist")
+        nc.vector.scalar_tensor_tensor(dist[:], cross[:], b_sq[:], shrink[:], ALU.add, ALU.mult)
+
+        dist_min = held.tile([N, 1], F32, name="dist_min")
+        nc.vector.tensor_reduce(dist_min[:], dist[:], mybir.AxisListType.X, ALU.min)
+        expd = held.tile([N, M], F32, name="expd")
+        exp_sum = held.tile([N, 1], F32, name="exp_sum")
+        nc.scalar.activation(expd[:], dist[:], FUNC.Exp, bias=dist_min[:], scale=-1.0, accum_out=exp_sum[:])
+        inv_sum = held.tile([N, 1], F32, name="inv_sum")
+        nc.vector.reciprocal(inv_sum[:], exp_sum[:])
+        aff = held.tile([N, M], BF16, name="aff")
+        nc.vector.tensor_scalar_mul(aff[:], expd[:], inv_sum[:])
+
+        aff_t_ps = psum.tile([P, SLOT_BLOCKS, N], BF16, name="aff_t_ps")
+        for b in range(SLOT_BLOCKS):
+            nc.tensor.transpose(aff_t_ps[:, b, :], aff[:, b * P : (b + 1) * P], ident[:])
+        aff_t = held.tile([P, SLOT_BLOCKS, N], BF16, name="aff_t")
+        nc.vector.tensor_copy(aff_t[:], aff_t_ps[:])
+
+        read = held.tile([P, VALUE_BLOCKS, N], F32, name="read")
+        for h in range(VALUE_BLOCKS):
+            read_ps = psum.tile([P, N], F32, name=f"read_ps{h}")
+            for b in range(SLOT_BLOCKS):
+                nc.tensor.matmul(
+                    read_ps[:],
+                    mv[:, b, h * P : (h + 1) * P],
+                    aff_t[:, b, :],
+                    start=(b == 0),
+                    stop=(b == SLOT_BLOCKS - 1),
+                )
+            nc.vector.tensor_copy(read[:, h, :], read_ps[:])
+            nc.sync.dma_start(out[h * P : (h + 1) * P, :], read[:, h, :])

@@ -27,16 +27,16 @@ def tile_xmem_kernel(
     ):
         offsets = held.tile([P, N // 16], U16, name="offsets")
         nc.sync.dma_start(offsets[:], offs)
+        sel = held.tile([CK, N], F32, name="sel")
+        nc.sync.dma_start(sel[:], query_selection)
+        mk = held.tile([CK, M], BF16, name="mk")
+        nc.sync.dma_start(mk[:], memory_key)
         keys = held.tile([CK, S], F32, name="keys")
         nc.sync.dma_start(keys[:], query_key)
-        sel = held.tile([CK, N], F32, name="sel")
-        nc.scalar.dma_start(sel[:], query_selection)
-        mk = held.tile([CK, M], BF16, name="mk")
-        nc.scalar.dma_start(mk[:], memory_key)
         shrink = held.tile([P, M], F32, name="shrink")
-        nc.sync.dma_start(shrink[:], memory_shrinkage.rearrange("m o -> (m o)").partition_broadcast(P))
+        nc.gpsimd.dma_start(shrink[:], memory_shrinkage.rearrange("m o -> (m o)").partition_broadcast(P))
         mv = held.tile([P, SLOT_BLOCKS, V], BF16, name="mv")
-        nc.scalar.dma_start(mv[:], memory_value.rearrange("(b p) v -> p b v", p=P))
+        nc.gpsimd.dma_start(mv[:], memory_value.rearrange("(b p) v -> p b v", p=P))
 
         ident = held.tile([P, P], BF16, name="ident")
         make_identity(nc, ident[:])

@@ -14,6 +14,9 @@ CK, S, N, M, V = 128, 512, 128, 512, 256
 SLOT_BLOCKS = M // P
 VALUE_BLOCKS = V // P
 
+WARM_LOADS = 6
+WARM_SOFTMAX = 4
+
 FLOPS = 2 * (2 * CK) * M * N + 2 * CK * N + 2 * M * V * N
 
 
@@ -40,8 +43,16 @@ def tile_xmem_kernel(
 
         ident = held.tile([P, P], BF16, name="ident")
         make_identity(nc, ident[:])
-        ones = held.tile([CK, 1], F32, name="ones")
+        ident_f = held.tile([P, P], F32, name="ident_f")
+        make_identity(nc, ident_f[:])
+        ones = held.tile([P, P], F32, name="ones")
         nc.vector.memset(ones[:], 1.0)
+
+        zeros = held.tile([P, M], BF16, name="zeros")
+        nc.vector.memset(zeros[:], 0.0)
+        unread = psum.tile([P, M], F32, name="unread")
+        for i in range(WARM_LOADS):
+            nc.tensor.matmul(unread[:], zeros[:, 0:P], zeros[:], start=True, stop=True)
 
         sel_k = held.tile([CK, N], F32, name="sel_k")
         nc.vector.tensor_scalar_mul(sel_k[:], sel[:], 1.0 / math.sqrt(CK))
@@ -61,37 +72,47 @@ def tile_xmem_kernel(
         nc.tensor.matmul(cross[:], sel_bf[:], mk_sq[:], start=True, stop=False)
         nc.tensor.matmul(cross[:], qs_m2[:], mk[:], start=False, stop=True)
         b_sq = psum.tile([N, 1], F32, name="b_sq")
-        nc.tensor.matmul(b_sq[:], qqs[:], ones[:], start=True, stop=True)
+        nc.tensor.matmul(b_sq[:], qqs[:], ones[:, 0:1], start=True, stop=True)
+
+        for i in range(WARM_SOFTMAX):
+            nc.tensor.matmul(unread[:], qs_m2[:], mk[:], start=True, stop=True)
 
         dist = held.tile([N, M], F32, name="dist")
         nc.vector.scalar_tensor_tensor(dist[:], cross[:], b_sq[:], shrink[:], ALU.add, ALU.mult)
 
         dist_min = held.tile([N, 1], F32, name="dist_min")
         nc.vector.tensor_reduce(dist_min[:], dist[:], mybir.AxisListType.X, ALU.min)
-        expd = held.tile([N, M], F32, name="expd")
+        expd = held.tile([N, M], BF16, name="expd")
         exp_sum = held.tile([N, 1], F32, name="exp_sum")
         nc.scalar.activation(expd[:], dist[:], FUNC.Exp, bias=dist_min[:], scale=-1.0, accum_out=exp_sum[:])
+
+        expd_t_ps = psum.tile([P, SLOT_BLOCKS, N], BF16, name="expd_t_ps")
+        for b in range(SLOT_BLOCKS):
+            nc.tensor.transpose(expd_t_ps[:, b, :], expd[:, b * P : (b + 1) * P], ident[:])
+        expd_t = held.tile([P, SLOT_BLOCKS, N], BF16, name="expd_t")
+        nc.vector.tensor_copy(expd_t[:], expd_t_ps[:])
+
         inv_sum = held.tile([N, 1], F32, name="inv_sum")
         nc.vector.reciprocal(inv_sum[:], exp_sum[:])
-        aff = held.tile([N, M], BF16, name="aff")
-        nc.vector.tensor_scalar_mul(aff[:], expd[:], inv_sum[:])
-
-        aff_t_ps = psum.tile([P, SLOT_BLOCKS, N], BF16, name="aff_t_ps")
-        for b in range(SLOT_BLOCKS):
-            nc.tensor.transpose(aff_t_ps[:, b, :], aff[:, b * P : (b + 1) * P], ident[:])
-        aff_t = held.tile([P, SLOT_BLOCKS, N], BF16, name="aff_t")
-        nc.vector.tensor_copy(aff_t[:], aff_t_ps[:])
+        inv_diag = held.tile([N, N], F32, name="inv_diag")
+        nc.vector.tensor_scalar_mul(inv_diag[:], ident_f[:], inv_sum[:])
+        inv_rows_ps = psum.tile([P, N], F32, name="inv_rows_ps")
+        nc.tensor.matmul(inv_rows_ps[:], ones[:], inv_diag[:], start=True, stop=True)
+        inv_rows = held.tile([P, N], F32, name="inv_rows")
+        nc.scalar.copy(inv_rows[:], inv_rows_ps[:])
 
         read = held.tile([P, VALUE_BLOCKS, N], F32, name="read")
+        read_ps = [psum.tile([P, N], F32, name=f"read_ps{h}") for h in range(VALUE_BLOCKS)]
         for h in range(VALUE_BLOCKS):
-            read_ps = psum.tile([P, N], F32, name=f"read_ps{h}")
             for b in range(SLOT_BLOCKS):
                 nc.tensor.matmul(
-                    read_ps[:],
+                    read_ps[h][:],
                     mv[:, b, h * P : (h + 1) * P],
-                    aff_t[:, b, :],
+                    expd_t[:, b, :],
                     start=(b == 0),
                     stop=(b == SLOT_BLOCKS - 1),
                 )
-            nc.vector.tensor_copy(read[:, h, :], read_ps[:])
-            nc.sync.dma_start(out[h * P : (h + 1) * P, :], read[:, h, :])
+        stores = [nc.sync, nc.scalar]
+        for h in range(VALUE_BLOCKS):
+            nc.vector.tensor_tensor(read[:, h, :], read_ps[h][:], inv_rows[:], ALU.mult)
+            stores[h].dma_start(out[h * P : (h + 1) * P, :], read[:, h, :])

@@ -14,9 +14,6 @@ CK, S, N, M, V = 128, 512, 128, 512, 256
 SLOT_BLOCKS = M // P
 VALUE_BLOCKS = V // P
 
-WARM_LOADS = 6
-WARM_SOFTMAX = 4
-
 FLOPS = 2 * (2 * CK) * M * N + 2 * CK * N + 2 * M * V * N
 
 
@@ -48,12 +45,6 @@ def tile_xmem_kernel(
         ones = held.tile([P, P], F32, name="ones")
         nc.vector.memset(ones[:], 1.0)
 
-        zeros = held.tile([P, M], BF16, name="zeros")
-        nc.vector.memset(zeros[:], 0.0)
-        unread = psum.tile([P, M], F32, name="unread")
-        for i in range(WARM_LOADS):
-            nc.tensor.matmul(unread[:], zeros[:, 0:P], zeros[:], start=True, stop=True)
-
         sel_k = held.tile([CK, N], F32, name="sel_k")
         nc.vector.tensor_scalar_mul(sel_k[:], sel[:], 1.0 / math.sqrt(CK))
         sel_bf = held.tile([CK, N], BF16, name="sel_bf")
@@ -73,9 +64,6 @@ def tile_xmem_kernel(
         nc.tensor.matmul(cross[:], qs_m2[:], mk[:], start=False, stop=True)
         b_sq = psum.tile([N, 1], F32, name="b_sq")
         nc.tensor.matmul(b_sq[:], qqs[:], ones[:, 0:1], start=True, stop=True)
-
-        for i in range(WARM_SOFTMAX):
-            nc.tensor.matmul(unread[:], qs_m2[:], mk[:], start=True, stop=True)
 
         dist = held.tile([N, M], F32, name="dist")
         nc.vector.scalar_tensor_tensor(dist[:], cross[:], b_sq[:], shrink[:], ALU.add, ALU.mult)

@@ -34,9 +34,9 @@ def tile_xmem_kernel(
         keys = held.tile([CK, S], F32, name="keys")
         nc.sync.dma_start(keys[:], query_key)
         shrink = held.tile([P, M], F32, name="shrink")
-        nc.gpsimd.dma_start(shrink[:], memory_shrinkage.rearrange("m o -> (m o)").partition_broadcast(P))
+        nc.sync.dma_start(shrink[:], memory_shrinkage.rearrange("m o -> (m o)").partition_broadcast(P))
         mv = held.tile([P, SLOT_BLOCKS, V], BF16, name="mv")
-        nc.gpsimd.dma_start(mv[:], memory_value.rearrange("(b p) v -> p b v", p=P))
+        nc.sync.dma_start(mv[:], memory_value.rearrange("(b p) v -> p b v", p=P))
 
         ident = held.tile([P, P], BF16, name="ident")
         make_identity(nc, ident[:])

@@ -13,6 +13,8 @@ P = 128
 CK, S, N, M, V = 128, 512, 128, 512, 256
 SLOT_BLOCKS = M // P
 VALUE_BLOCKS = V // P
+PAIR = 2
+PAIRS = SLOT_BLOCKS // PAIR
 
 FLOPS = 2 * (2 * CK) * M * N + 2 * CK * N + 2 * M * V * N
 
@@ -48,16 +50,16 @@ def tile_xmem_kernel(
         sel_k = held.tile([CK, N], F32, name="sel_k")
         nc.vector.tensor_scalar_mul(sel_k[:], sel[:], 1.0 / math.sqrt(CK))
         sel_bf = held.tile([CK, N], BF16, name="sel_bf")
-        nc.scalar.copy(sel_bf[:], sel_k[:])
+        nc.vector.tensor_copy(sel_bf[:], sel_k[:])
         mk_sq = held.tile([CK, M], BF16, name="mk_sq")
         nc.vector.tensor_tensor(mk_sq[:], mk[:], mk[:], ALU.mult)
 
         qs = held.tile([CK, N], F32, name="qs")
         nc.vector.tensor_tensor(qs[:], keys[:].indirect(offsets[:]), sel_k[:], ALU.mult)
+        qs_m2 = held.tile([CK, N], BF16, name="qs_m2")
+        nc.vector.tensor_scalar_mul(qs_m2[:], qs[:], -2.0)
         qqs = held.tile([CK, N], F32, name="qqs")
         nc.vector.tensor_tensor(qqs[:], keys[:].indirect(offsets[:]), qs[:], ALU.mult)
-        qs_m2 = held.tile([CK, N], BF16, name="qs_m2")
-        nc.scalar.mul(qs_m2[:], qs[:], -2.0)
 
         cross = psum.tile([N, M], F32, name="cross")
         nc.tensor.matmul(cross[:], sel_bf[:], mk_sq[:], start=True, stop=False)
@@ -74,32 +76,34 @@ def tile_xmem_kernel(
         exp_sum = held.tile([N, 1], F32, name="exp_sum")
         nc.scalar.activation(expd[:], dist[:], FUNC.Exp, bias=dist_min[:], scale=-1.0, accum_out=exp_sum[:])
 
-        expd_t_ps = psum.tile([P, SLOT_BLOCKS, N], BF16, name="expd_t_ps")
+        expd_t_ps = [psum.tile([P, PAIR, N], BF16, name=f"expd_t_ps{g}") for g in range(PAIRS)]
         for b in range(SLOT_BLOCKS):
-            nc.tensor.transpose(expd_t_ps[:, b, :], expd[:, b * P : (b + 1) * P], ident[:])
-        expd_t = held.tile([P, SLOT_BLOCKS, N], BF16, name="expd_t")
-        nc.vector.tensor_copy(expd_t[:], expd_t_ps[:])
+            nc.tensor.transpose(expd_t_ps[b // PAIR][:, b % PAIR, :], expd[:, b * P : (b + 1) * P], ident[:])
+        expd_t = [held.tile([P, PAIR, N], BF16, name=f"expd_t{g}") for g in range(PAIRS)]
+        nc.vector.tensor_copy(expd_t[0][:], expd_t_ps[0][:])
+        nc.scalar.copy(expd_t[1][:], expd_t_ps[1][:])
 
         inv_sum = held.tile([N, 1], F32, name="inv_sum")
         nc.vector.reciprocal(inv_sum[:], exp_sum[:])
-        inv_diag = held.tile([N, N], F32, name="inv_diag")
-        nc.vector.tensor_scalar_mul(inv_diag[:], ident_f[:], inv_sum[:])
+        inv_cols = held.tile([N, P], F32, name="inv_cols")
+        nc.vector.tensor_scalar_mul(inv_cols[:], ones[:], inv_sum[:])
         inv_rows_ps = psum.tile([P, N], F32, name="inv_rows_ps")
-        nc.tensor.matmul(inv_rows_ps[:], ones[:], inv_diag[:], start=True, stop=True)
+        nc.tensor.transpose(inv_rows_ps[:], inv_cols[:], ident_f[:])
         inv_rows = held.tile([P, N], F32, name="inv_rows")
         nc.scalar.copy(inv_rows[:], inv_rows_ps[:])
 
-        read = held.tile([P, VALUE_BLOCKS, N], F32, name="read")
         read_ps = [psum.tile([P, N], F32, name=f"read_ps{h}") for h in range(VALUE_BLOCKS)]
-        for h in range(VALUE_BLOCKS):
-            for b in range(SLOT_BLOCKS):
-                nc.tensor.matmul(
-                    read_ps[h][:],
-                    mv[:, b, h * P : (h + 1) * P],
-                    expd_t[:, b, :],
-                    start=(b == 0),
-                    stop=(b == SLOT_BLOCKS - 1),
-                )
+        for g in range(PAIRS):
+            for h in range(VALUE_BLOCKS):
+                for b in range(g * PAIR, (g + 1) * PAIR):
+                    nc.tensor.matmul(
+                        read_ps[h][:],
+                        mv[:, b, h * P : (h + 1) * P],
+                        expd_t[g][:, b % PAIR, :],
+                        start=(b == 0),
+                        stop=(b == SLOT_BLOCKS - 1),
+                    )
+        read = held.tile([P, VALUE_BLOCKS, N], F32, name="read")
         stores = [nc.sync, nc.scalar]
         for h in range(VALUE_BLOCKS):
             nc.vector.tensor_tensor(read[:, h, :], read_ps[h][:], inv_rows[:], ALU.mult)

@@ -29,14 +29,14 @@ def tile_xmem_kernel(
     ):
         offsets = held.tile([P, N // 16], U16, name="offsets")
         nc.sync.dma_start(offsets[:], offs)
+        shrink_col = held.tile([P, SLOT_BLOCKS], F32, name="shrink_col")
+        nc.sync.dma_start(shrink_col[:], memory_shrinkage.rearrange("(p b) o -> p (b o)", b=SLOT_BLOCKS))
         sel = held.tile([CK, N], F32, name="sel")
         nc.sync.dma_start(sel[:], query_selection)
         mk = held.tile([CK, M], BF16, name="mk")
         nc.sync.dma_start(mk[:], memory_key)
         keys = held.tile([CK, S], F32, name="keys")
         nc.sync.dma_start(keys[:], query_key)
-        shrink = held.tile([P, M], F32, name="shrink")
-        nc.sync.dma_start(shrink[:], memory_shrinkage.rearrange("m o -> (m o)").partition_broadcast(P))
         mv = held.tile([P, SLOT_BLOCKS, V], BF16, name="mv")
         nc.sync.dma_start(mv[:], memory_value.rearrange("(b p) v -> p b v", p=P))
 
@@ -46,6 +46,14 @@ def tile_xmem_kernel(
         make_identity(nc, ident_f[:])
         ones = held.tile([P, P], F32, name="ones")
         nc.vector.memset(ones[:], 1.0)
+
+        shrink_wide = held.tile([P, SLOT_BLOCKS, P], F32, name="shrink_wide")
+        nc.scalar.copy(shrink_wide[:], shrink_col[:].unsqueeze(2).to_broadcast([P, SLOT_BLOCKS, P]))
+        shrink_ps = psum.tile([P, SLOT_BLOCKS, P], F32, name="shrink_ps")
+        for b in range(SLOT_BLOCKS):
+            nc.tensor.transpose(shrink_ps[:, b, :], shrink_wide[:, b, :], ident_f[:])
+        shrink = held.tile([P, P, SLOT_BLOCKS], F32, name="shrink")
+        nc.scalar.copy(shrink[:], shrink_ps[:].rearrange("j b p -> j p b"))
 
         sel_k = held.tile([CK, N], F32, name="sel_k")
         nc.vector.tensor_scalar_mul(sel_k[:], sel[:], 1.0 / math.sqrt(CK))
@@ -68,7 +76,9 @@ def tile_xmem_kernel(
         nc.tensor.matmul(b_sq[:], qqs[:], ones[:, 0:1], start=True, stop=True)
 
         dist = held.tile([N, M], F32, name="dist")
-        nc.vector.scalar_tensor_tensor(dist[:], cross[:], b_sq[:], shrink[:], ALU.add, ALU.mult)
+        nc.vector.scalar_tensor_tensor(
+            dist[:], cross[:], b_sq[:], shrink[:].rearrange("j p b -> j (p b)"), ALU.add, ALU.mult
+        )
 
         dist_min = held.tile([N, 1], F32, name="dist_min")
         nc.vector.tensor_reduce(dist_min[:], dist[:], mybir.AxisListType.X, ALU.min)

@@ -29,14 +29,14 @@ def tile_xmem_kernel(
     ):
         offsets = held.tile([P, N // 16], U16, name="offsets")
         nc.sync.dma_start(offsets[:], offs)
-        shrink_col = held.tile([P, SLOT_BLOCKS], F32, name="shrink_col")
-        nc.sync.dma_start(shrink_col[:], memory_shrinkage.rearrange("(p b) o -> p (b o)", b=SLOT_BLOCKS))
         sel = held.tile([CK, N], F32, name="sel")
         nc.sync.dma_start(sel[:], query_selection)
         mk = held.tile([CK, M], BF16, name="mk")
         nc.sync.dma_start(mk[:], memory_key)
         keys = held.tile([CK, S], F32, name="keys")
         nc.sync.dma_start(keys[:], query_key)
+        shrink = held.tile([P, M], F32, name="shrink")
+        nc.sync.dma_start(shrink[:], memory_shrinkage.rearrange("m o -> (m o)").partition_broadcast(P))
         mv = held.tile([P, SLOT_BLOCKS, V], BF16, name="mv")
         nc.sync.dma_start(mv[:], memory_value.rearrange("(b p) v -> p b v", p=P))
 
@@ -46,14 +46,8 @@ def tile_xmem_kernel(
         make_identity(nc, ident_f[:])
         ones = held.tile([P, P], F32, name="ones")
         nc.vector.memset(ones[:], 1.0)
-
-        shrink_wide = held.tile([P, SLOT_BLOCKS, P], F32, name="shrink_wide")
-        nc.scalar.copy(shrink_wide[:], shrink_col[:].unsqueeze(2).to_broadcast([P, SLOT_BLOCKS, P]))
-        shrink_ps = psum.tile([P, SLOT_BLOCKS, P], F32, name="shrink_ps")
-        for b in range(SLOT_BLOCKS):
-            nc.tensor.transpose(shrink_ps[:, b, :], shrink_wide[:, b, :], ident_f[:])
-        shrink = held.tile([P, P, SLOT_BLOCKS], F32, name="shrink")
-        nc.scalar.copy(shrink[:], shrink_ps[:].rearrange("j b p -> j p b"))
+        ones_bf = held.tile([CK, 1], BF16, name="ones_bf")
+        nc.vector.memset(ones_bf[:], 1.0)
 
         sel_k = held.tile([CK, N], F32, name="sel_k")
         nc.vector.tensor_scalar_mul(sel_k[:], sel[:], 1.0 / math.sqrt(CK))
@@ -68,17 +62,17 @@ def tile_xmem_kernel(
         nc.vector.tensor_scalar_mul(qs_m2[:], qs[:], -2.0)
         qqs = held.tile([CK, N], F32, name="qqs")
         nc.vector.tensor_tensor(qqs[:], keys[:].indirect(offsets[:]), qs[:], ALU.mult)
+        qqs_bf = held.tile([CK, N], BF16, name="qqs_bf")
+        nc.vector.tensor_copy(qqs_bf[:], qqs[:])
 
         cross = psum.tile([N, M], F32, name="cross")
         nc.tensor.matmul(cross[:], sel_bf[:], mk_sq[:], start=True, stop=False)
         nc.tensor.matmul(cross[:], qs_m2[:], mk[:], start=False, stop=True)
         b_sq = psum.tile([N, 1], F32, name="b_sq")
-        nc.tensor.matmul(b_sq[:], qqs[:], ones[:, 0:1], start=True, stop=True)
+        nc.tensor.matmul(b_sq[:], qqs_bf[:], ones_bf[:], start=True, stop=True)
 
         dist = held.tile([N, M], F32, name="dist")
-        nc.vector.scalar_tensor_tensor(
-            dist[:], cross[:], b_sq[:], shrink[:].rearrange("j p b -> j (p b)"), ALU.add, ALU.mult
-        )
+        nc.vector.scalar_tensor_tensor(dist[:], cross[:], b_sq[:], shrink[:], ALU.add, ALU.mult)
 
         dist_min = held.tile([N, 1], F32, name="dist_min")
         nc.vector.tensor_reduce(dist_min[:], dist[:], mybir.AxisListType.X, ALU.min)

@@ -1,7 +1,6 @@
 import math
 
 import concourse.mybir as mybir
-from concourse.masks import make_identity
 
 F32 = mybir.dt.float32
 BF16 = mybir.dt.bfloat16
@@ -13,8 +12,6 @@ P = 128
 CK, S, N, M, V = 128, 512, 128, 512, 256
 SLOT_BLOCKS = M // P
 VALUE_BLOCKS = V // P
-PAIR = 2
-PAIRS = SLOT_BLOCKS // PAIR
 
 FLOPS = 2 * (2 * CK) * M * N + 2 * CK * N + 2 * M * V * N
 
@@ -35,80 +32,55 @@ def tile_xmem_kernel(
         nc.sync.dma_start(mk[:], memory_key)
         keys = held.tile([CK, S], F32, name="keys")
         nc.sync.dma_start(keys[:], query_key)
-        shrink = held.tile([P, M], F32, name="shrink")
-        nc.sync.dma_start(shrink[:], memory_shrinkage.rearrange("m o -> (m o)").partition_broadcast(P))
+        shrink = held.tile([P, SLOT_BLOCKS], F32, name="shrink")
+        nc.sync.dma_start(shrink[:], memory_shrinkage.rearrange("(b p) o -> p (b o)", p=P))
         mv = held.tile([P, SLOT_BLOCKS, V], BF16, name="mv")
         nc.sync.dma_start(mv[:], memory_value.rearrange("(b p) v -> p b v", p=P))
 
-        ident = held.tile([P, P], BF16, name="ident")
-        make_identity(nc, ident[:])
-        ident_f = held.tile([P, P], F32, name="ident_f")
-        make_identity(nc, ident_f[:])
-        ones = held.tile([P, P], F32, name="ones")
+        minus_ones = held.tile([CK, P], BF16, name="minus_ones")
+        nc.vector.memset(minus_ones[:], -1.0)
+        ones = held.tile([P, P], BF16, name="ones")
         nc.vector.memset(ones[:], 1.0)
-        ones_bf = held.tile([CK, 1], BF16, name="ones_bf")
-        nc.vector.memset(ones_bf[:], 1.0)
 
-        sel_k = held.tile([CK, N], F32, name="sel_k")
-        nc.vector.tensor_scalar_mul(sel_k[:], sel[:], 1.0 / math.sqrt(CK))
-        sel_bf = held.tile([CK, N], BF16, name="sel_bf")
-        nc.vector.tensor_copy(sel_bf[:], sel_k[:])
+        sel_neg = held.tile([CK, N], BF16, name="sel_neg")
+        nc.vector.tensor_scalar_mul(sel_neg[:], sel[:], -1.0)
         mk_sq = held.tile([CK, M], BF16, name="mk_sq")
         nc.vector.tensor_tensor(mk_sq[:], mk[:], mk[:], ALU.mult)
+        exp_scale = held.tile([P, SLOT_BLOCKS], F32, name="exp_scale")
+        nc.vector.tensor_scalar_mul(exp_scale[:], shrink[:], 1.0 / math.sqrt(CK))
+
+        dist_ps = [psum.tile([P, N], F32, name=f"dist_ps{b}") for b in range(SLOT_BLOCKS)]
+        for b in range(SLOT_BLOCKS):
+            nc.tensor.matmul(dist_ps[b][:], mk_sq[:, b * P : (b + 1) * P], sel_neg[:], start=True, stop=False)
 
         qs = held.tile([CK, N], F32, name="qs")
-        nc.vector.tensor_tensor(qs[:], keys[:].indirect(offsets[:]), sel_k[:], ALU.mult)
-        qs_m2 = held.tile([CK, N], BF16, name="qs_m2")
-        nc.vector.tensor_scalar_mul(qs_m2[:], qs[:], -2.0)
+        nc.vector.tensor_tensor(qs[:], keys[:].indirect(offsets[:]), sel[:], ALU.mult)
+        qs_x2 = held.tile([CK, N], BF16, name="qs_x2")
+        nc.vector.tensor_scalar_mul(qs_x2[:], qs[:], 2.0)
         qqs = held.tile([CK, N], F32, name="qqs")
         nc.vector.tensor_tensor(qqs[:], keys[:].indirect(offsets[:]), qs[:], ALU.mult)
         qqs_bf = held.tile([CK, N], BF16, name="qqs_bf")
         nc.vector.tensor_copy(qqs_bf[:], qqs[:])
 
-        cross = psum.tile([N, M], F32, name="cross")
-        nc.tensor.matmul(cross[:], sel_bf[:], mk_sq[:], start=True, stop=False)
-        nc.tensor.matmul(cross[:], qs_m2[:], mk[:], start=False, stop=True)
-        b_sq = psum.tile([N, 1], F32, name="b_sq")
-        nc.tensor.matmul(b_sq[:], qqs_bf[:], ones_bf[:], start=True, stop=True)
-
-        dist = held.tile([N, M], F32, name="dist")
-        nc.vector.scalar_tensor_tensor(dist[:], cross[:], b_sq[:], shrink[:], ALU.add, ALU.mult)
-
-        dist_min = held.tile([N, 1], F32, name="dist_min")
-        nc.vector.tensor_reduce(dist_min[:], dist[:], mybir.AxisListType.X, ALU.min)
-        expd = held.tile([N, M], BF16, name="expd")
-        exp_sum = held.tile([N, 1], F32, name="exp_sum")
-        nc.scalar.activation(expd[:], dist[:], FUNC.Exp, bias=dist_min[:], scale=-1.0, accum_out=exp_sum[:])
-
-        expd_t_ps = [psum.tile([P, PAIR, N], BF16, name=f"expd_t_ps{g}") for g in range(PAIRS)]
         for b in range(SLOT_BLOCKS):
-            nc.tensor.transpose(expd_t_ps[b // PAIR][:, b % PAIR, :], expd[:, b * P : (b + 1) * P], ident[:])
-        expd_t = [held.tile([P, PAIR, N], BF16, name=f"expd_t{g}") for g in range(PAIRS)]
-        nc.vector.tensor_copy(expd_t[0][:], expd_t_ps[0][:])
-        nc.scalar.copy(expd_t[1][:], expd_t_ps[1][:])
+            nc.tensor.matmul(dist_ps[b][:], mk[:, b * P : (b + 1) * P], qs_x2[:], start=False, stop=False)
+        for b in range(SLOT_BLOCKS):
+            nc.tensor.matmul(dist_ps[b][:], minus_ones[:], qqs_bf[:], start=False, stop=True)
 
-        inv_sum = held.tile([N, 1], F32, name="inv_sum")
-        nc.vector.reciprocal(inv_sum[:], exp_sum[:])
-        inv_cols = held.tile([N, P], F32, name="inv_cols")
-        nc.vector.tensor_scalar_mul(inv_cols[:], ones[:], inv_sum[:])
-        inv_rows_ps = psum.tile([P, N], F32, name="inv_rows_ps")
-        nc.tensor.transpose(inv_rows_ps[:], inv_cols[:], ident_f[:])
-        inv_rows = held.tile([P, N], F32, name="inv_rows")
-        nc.scalar.copy(inv_rows[:], inv_rows_ps[:])
-
+        sum_ps = psum.tile([P, N], F32, name="sum_ps")
         read_ps = [psum.tile([P, N], F32, name=f"read_ps{h}") for h in range(VALUE_BLOCKS)]
-        for g in range(PAIRS):
+        for b in range(SLOT_BLOCKS):
+            first, last = b == 0, b == SLOT_BLOCKS - 1
+            expd = held.tile([P, N], BF16, name=f"expd{b}")
+            nc.scalar.activation(expd[:], dist_ps[b][:], FUNC.Exp, scale=exp_scale[:, b : b + 1])
+            nc.tensor.matmul(sum_ps[:], ones[:], expd[:], start=first, stop=last)
             for h in range(VALUE_BLOCKS):
-                for b in range(g * PAIR, (g + 1) * PAIR):
-                    nc.tensor.matmul(
-                        read_ps[h][:],
-                        mv[:, b, h * P : (h + 1) * P],
-                        expd_t[g][:, b % PAIR, :],
-                        start=(b == 0),
-                        stop=(b == SLOT_BLOCKS - 1),
-                    )
+                nc.tensor.matmul(read_ps[h][:], mv[:, b, h * P : (h + 1) * P], expd[:], start=first, stop=last)
+
+        inv_sum = held.tile([P, N], F32, name="inv_sum")
+        nc.vector.reciprocal(inv_sum[:], sum_ps[:])
         read = held.tile([P, VALUE_BLOCKS, N], F32, name="read")
         stores = [nc.sync, nc.scalar]
         for h in range(VALUE_BLOCKS):
-            nc.vector.tensor_tensor(read[:, h, :], read_ps[h][:], inv_rows[:], ALU.mult)
+            nc.vector.tensor_tensor(read[:, h, :], read_ps[h][:], inv_sum[:], ALU.mult)
             stores[h].dma_start(out[h * P : (h + 1) * P, :], read[:, h, :])

@@ -12,6 +12,8 @@ P = 128
 CK, S, N, M, V = 128, 512, 128, 512, 256
 SLOT_BLOCKS = M // P
 VALUE_BLOCKS = V // P
+HALVES = 2
+HALF = N // HALVES
 
 FLOPS = 2 * (2 * CK) * M * N + 2 * CK * N + 2 * M * V * N
 
@@ -67,18 +69,22 @@ def tile_xmem_kernel(
         for b in range(SLOT_BLOCKS):
             nc.tensor.matmul(dist_ps[b][:], minus_ones[:], qqs_bf[:], start=False, stop=True)
 
-        sum_ps = psum.tile([P, N], F32, name="sum_ps")
+        sum_ps = [psum.tile([P, HALF], F32, name=f"sum_ps{g}") for g in range(HALVES)]
         read_ps = [psum.tile([P, N], F32, name=f"read_ps{h}") for h in range(VALUE_BLOCKS)]
-        for b in range(SLOT_BLOCKS):
-            first, last = b == 0, b == SLOT_BLOCKS - 1
-            expd = held.tile([P, N], BF16, name=f"expd{b}")
-            nc.scalar.activation(expd[:], dist_ps[b][:], FUNC.Exp, scale=exp_scale[:, b : b + 1])
-            nc.tensor.matmul(sum_ps[:], ones[:], expd[:], start=first, stop=last)
-            for h in range(VALUE_BLOCKS):
-                nc.tensor.matmul(read_ps[h][:], mv[:, b, h * P : (h + 1) * P], expd[:], start=first, stop=last)
-
+        expd = [held.tile([P, N], BF16, name=f"expd{b}") for b in range(SLOT_BLOCKS)]
         inv_sum = held.tile([P, N], F32, name="inv_sum")
-        nc.vector.reciprocal(inv_sum[:], sum_ps[:])
+        for g in range(HALVES):
+            cols = slice(g * HALF, (g + 1) * HALF)
+            for b in range(SLOT_BLOCKS):
+                first, last = b == 0, b == SLOT_BLOCKS - 1
+                nc.scalar.activation(expd[b][:, cols], dist_ps[b][:, cols], FUNC.Exp, scale=exp_scale[:, b : b + 1])
+                nc.tensor.matmul(sum_ps[g][:], ones[:], expd[b][:, cols], start=first, stop=last)
+                for h in range(VALUE_BLOCKS):
+                    nc.tensor.matmul(
+                        read_ps[h][:, cols], mv[:, b, h * P : (h + 1) * P], expd[b][:, cols], start=first, stop=last
+                    )
+            nc.vector.reciprocal(inv_sum[:, cols], sum_ps[g][:])
+
         read = held.tile([P, VALUE_BLOCKS, N], F32, name="read")
         stores = [nc.sync, nc.scalar]
         for h in range(VALUE_BLOCKS):

@@ -79,11 +79,13 @@ def tile_xmem_kernel(
                 first, last = b == 0, b == SLOT_BLOCKS - 1
                 nc.scalar.activation(expd[b][:, cols], dist_ps[b][:, cols], FUNC.Exp, scale=exp_scale[:, b : b + 1])
                 nc.tensor.matmul(sum_ps[g][:], ones[:], expd[b][:, cols], start=first, stop=last)
+            nc.vector.reciprocal(inv_sum[:, cols], sum_ps[g][:])
+            for b in range(SLOT_BLOCKS):
+                first, last = b == 0, b == SLOT_BLOCKS - 1
                 for h in range(VALUE_BLOCKS):
                     nc.tensor.matmul(
                         read_ps[h][:, cols], mv[:, b, h * P : (h + 1) * P], expd[b][:, cols], start=first, stop=last
                     )
-            nc.vector.reciprocal(inv_sum[:, cols], sum_ps[g][:])
 
         read = held.tile([P, VALUE_BLOCKS, N], F32, name="read")
         stores = [nc.sync, nc.scalar]

@@ -56,13 +56,19 @@ def tile_xmem_kernel(
             nc.tensor.matmul(dist_ps[b][:], mk_sq[:, b * P : (b + 1) * P], sel_neg[:], start=True, stop=False)
 
         qs = held.tile([CK, N], F32, name="qs")
-        nc.vector.tensor_tensor(qs[:], keys[:].indirect(offsets[:]), sel[:], ALU.mult)
         qs_x2 = held.tile([CK, N], BF16, name="qs_x2")
-        nc.vector.tensor_scalar_mul(qs_x2[:], qs[:], 2.0)
         qqs = held.tile([CK, N], F32, name="qqs")
-        nc.vector.tensor_tensor(qqs[:], keys[:].indirect(offsets[:]), qs[:], ALU.mult)
         qqs_bf = held.tile([CK, N], BF16, name="qqs_bf")
-        nc.vector.tensor_copy(qqs_bf[:], qqs[:])
+        halves = [slice(g * HALF, (g + 1) * HALF) for g in range(HALVES)]
+        picked = [keys[:].indirect(offsets[:, g * (HALF // 16) : (g + 1) * (HALF // 16)]) for g in range(HALVES)]
+        for g in range(HALVES):
+            nc.vector.tensor_tensor(qs[:, halves[g]], picked[g], sel[:, halves[g]], ALU.mult)
+        for g in range(HALVES):
+            nc.vector.tensor_scalar_mul(qs_x2[:, halves[g]], qs[:, halves[g]], 2.0)
+        for g in range(HALVES):
+            nc.vector.tensor_tensor(qqs[:, halves[g]], picked[g], qs[:, halves[g]], ALU.mult)
+        for g in range(HALVES):
+            nc.vector.tensor_copy(qqs_bf[:, halves[g]], qqs[:, halves[g]])
 
         for b in range(SLOT_BLOCKS):
             nc.tensor.matmul(dist_ps[b][:], mk[:, b * P : (b + 1) * P], qs_x2[:], start=False, stop=False)

@@ -51,50 +51,59 @@ def tile_xmem_kernel(
         exp_scale = held.tile([P, SLOT_BLOCKS], F32, name="exp_scale")
         nc.vector.tensor_scalar_mul(exp_scale[:], shrink[:], 1.0 / math.sqrt(CK))
 
-        dist_ps = [psum.tile([P, N], F32, name=f"dist_ps{b}") for b in range(SLOT_BLOCKS)]
-        for b in range(SLOT_BLOCKS):
-            nc.tensor.matmul(dist_ps[b][:], mk_sq[:, b * P : (b + 1) * P], sel_neg[:], start=True, stop=False)
+        halves = [slice(g * HALF, (g + 1) * HALF) for g in range(HALVES)]
+        blocks = [slice(b * P, (b + 1) * P) for b in range(SLOT_BLOCKS)]
+
+        dist_ps = [
+            [psum.tile([P, HALF], F32, name=f"dist_ps{g}_{b}", tag=f"bank{g}_{b}") for b in range(SLOT_BLOCKS)]
+            for g in range(HALVES)
+        ]
+        for g in range(HALVES):
+            for b in range(SLOT_BLOCKS):
+                nc.tensor.matmul(dist_ps[g][b][:], mk_sq[:, blocks[b]], sel_neg[:, halves[g]], start=True, stop=False)
 
         qs = held.tile([CK, N], F32, name="qs")
         qs_x2 = held.tile([CK, N], BF16, name="qs_x2")
         qqs = held.tile([CK, N], F32, name="qqs")
         qqs_bf = held.tile([CK, N], BF16, name="qqs_bf")
-        halves = [slice(g * HALF, (g + 1) * HALF) for g in range(HALVES)]
         picked = [keys[:].indirect(offsets[:, g * (HALF // 16) : (g + 1) * (HALF // 16)]) for g in range(HALVES)]
-        for g in range(HALVES):
-            nc.vector.tensor_tensor(qs[:, halves[g]], picked[g], sel[:, halves[g]], ALU.mult)
-        for g in range(HALVES):
-            nc.vector.tensor_scalar_mul(qs_x2[:, halves[g]], qs[:, halves[g]], 2.0)
-        for g in range(HALVES):
-            nc.vector.tensor_tensor(qqs[:, halves[g]], picked[g], qs[:, halves[g]], ALU.mult)
-        for g in range(HALVES):
-            nc.vector.tensor_copy(qqs_bf[:, halves[g]], qqs[:, halves[g]])
+        first, second = halves
+        nc.vector.tensor_tensor(qs[:, first], picked[0], sel[:, first], ALU.mult)
+        nc.vector.tensor_tensor(qs[:, second], picked[1], sel[:, second], ALU.mult)
+        nc.vector.tensor_scalar_mul(qs_x2[:, first], qs[:, first], 2.0)
+        nc.vector.tensor_tensor(qqs[:, first], picked[0], qs[:, first], ALU.mult)
+        nc.vector.tensor_scalar_mul(qs_x2[:, second], qs[:, second], 2.0)
+        nc.vector.tensor_copy(qqs_bf[:, first], qqs[:, first])
+        nc.vector.tensor_tensor(qqs[:, second], picked[1], qs[:, second], ALU.mult)
+        nc.vector.tensor_copy(qqs_bf[:, second], qqs[:, second])
 
-        for b in range(SLOT_BLOCKS):
-            nc.tensor.matmul(dist_ps[b][:], mk[:, b * P : (b + 1) * P], qs_x2[:], start=False, stop=False)
-        for b in range(SLOT_BLOCKS):
-            nc.tensor.matmul(dist_ps[b][:], minus_ones[:], qqs_bf[:], start=False, stop=True)
-
-        sum_ps = [psum.tile([P, HALF], F32, name=f"sum_ps{g}") for g in range(HALVES)]
-        read_ps = [psum.tile([P, N], F32, name=f"read_ps{h}") for h in range(VALUE_BLOCKS)]
-        expd = [held.tile([P, N], BF16, name=f"expd{b}") for b in range(SLOT_BLOCKS)]
-        inv_sum = held.tile([P, N], F32, name="inv_sum")
         for g in range(HALVES):
-            cols = slice(g * HALF, (g + 1) * HALF)
             for b in range(SLOT_BLOCKS):
-                first, last = b == 0, b == SLOT_BLOCKS - 1
-                nc.scalar.activation(expd[b][:, cols], dist_ps[b][:, cols], FUNC.Exp, scale=exp_scale[:, b : b + 1])
-                nc.tensor.matmul(sum_ps[g][:], ones[:], expd[b][:, cols], start=first, stop=last)
-            nc.vector.reciprocal(inv_sum[:, cols], sum_ps[g][:])
+                nc.tensor.matmul(dist_ps[g][b][:], mk[:, blocks[b]], qs_x2[:, halves[g]], start=False, stop=False)
             for b in range(SLOT_BLOCKS):
-                first, last = b == 0, b == SLOT_BLOCKS - 1
-                for h in range(VALUE_BLOCKS):
+                nc.tensor.matmul(dist_ps[g][b][:], minus_ones[:], qqs_bf[:, halves[g]], start=False, stop=True)
+
+        out_by_block = out.rearrange("(h p) j -> p h j", p=P)
+        for g in range(HALVES):
+            expd = [held.tile([P, HALF], BF16, name=f"expd{g}_{b}") for b in range(SLOT_BLOCKS)]
+            sum_ps = psum.tile([P, HALF], F32, name=f"sum_ps{g}", tag=f"bank0_{2 * g}")
+            for b in range(SLOT_BLOCKS):
+                nc.scalar.activation(expd[b][:], dist_ps[g][b][:], FUNC.Exp, scale=exp_scale[:, b : b + 1])
+                nc.tensor.matmul(sum_ps[:], ones[:], expd[b][:], start=(b == 0), stop=(b == SLOT_BLOCKS - 1))
+            inv_sum = held.tile([P, 1, HALF], F32, name=f"inv_sum{g}")
+            nc.vector.reciprocal(inv_sum[:, 0, :], sum_ps[:])
+
+            read_ps = psum.tile([P, VALUE_BLOCKS, HALF], F32, name=f"read_ps{g}", tag=f"bank0_{2 * g + 1}")
+            for h in range(VALUE_BLOCKS):
+                for b in range(SLOT_BLOCKS):
                     nc.tensor.matmul(
-                        read_ps[h][:, cols], mv[:, b, h * P : (h + 1) * P], expd[b][:, cols], start=first, stop=last
+                        read_ps[:, h, :],
+                        mv[:, b, h * P : (h + 1) * P],
+                        expd[b][:],
+                        start=(b == 0),
+                        stop=(b == SLOT_BLOCKS - 1),
                     )
 
-        read = held.tile([P, VALUE_BLOCKS, N], F32, name="read")
-        stores = [nc.sync, nc.scalar]
-        for h in range(VALUE_BLOCKS):
-            nc.vector.tensor_tensor(read[:, h, :], read_ps[h][:], inv_sum[:], ALU.mult)
-            stores[h].dma_start(out[h * P : (h + 1) * P, :], read[:, h, :])
+            read = held.tile([P, VALUE_BLOCKS, HALF], F32, name=f"read{g}")
+            nc.vector.tensor_tensor(read[:], read_ps[:], inv_sum[:].to_broadcast([P, VALUE_BLOCKS, HALF]), ALU.mult)
+            nc.sync.dma_start(out_by_block[:, :, halves[g]], read[:])

@@ -35,9 +35,9 @@ def tile_xmem_kernel(
         keys = held.tile([CK, S], F32, name="keys")
         nc.sync.dma_start(keys[:], query_key)
         shrink = held.tile([P, SLOT_BLOCKS], F32, name="shrink")
-        nc.sync.dma_start(shrink[:], memory_shrinkage.rearrange("(b p) o -> p (b o)", p=P))
+        nc.sync.dma_start(shrink[:], memory_shrinkage.rearrange("(p b) o -> p (b o)", p=P))
         mv = held.tile([P, SLOT_BLOCKS, V], BF16, name="mv")
-        nc.sync.dma_start(mv[:], memory_value.rearrange("(b p) v -> p b v", p=P))
+        nc.sync.dma_start(mv[:], memory_value.rearrange("(p b) v -> p b v", p=P))
 
         minus_ones = held.tile([CK, P], BF16, name="minus_ones")
         nc.vector.memset(minus_ones[:], -1.0)
@@ -46,13 +46,15 @@ def tile_xmem_kernel(
 
         sel_neg = held.tile([CK, N], BF16, name="sel_neg")
         nc.vector.tensor_scalar_mul(sel_neg[:], sel[:], -1.0)
-        mk_sq = held.tile([CK, M], BF16, name="mk_sq")
-        nc.vector.tensor_tensor(mk_sq[:], mk[:], mk[:], ALU.mult)
+        mk_by_block = mk[:].rearrange("c (p b) -> c b p", b=SLOT_BLOCKS)
+        mk_sq = held.tile([CK, SLOT_BLOCKS, P], BF16, name="mk_sq")
+        nc.vector.tensor_tensor(mk_sq[:], mk_by_block, mk_by_block, ALU.mult)
+        mk_blocks = held.tile([CK, SLOT_BLOCKS, P], BF16, name="mk_blocks")
+        nc.scalar.copy(mk_blocks[:], mk_by_block)
         exp_scale = held.tile([P, SLOT_BLOCKS], F32, name="exp_scale")
         nc.vector.tensor_scalar_mul(exp_scale[:], shrink[:], 1.0 / math.sqrt(CK))
 
         halves = [slice(g * HALF, (g + 1) * HALF) for g in range(HALVES)]
-        blocks = [slice(b * P, (b + 1) * P) for b in range(SLOT_BLOCKS)]
 
         dist_ps = [
             [psum.tile([P, HALF], F32, name=f"dist_ps{g}_{b}", tag=f"bank{g}_{b}") for b in range(SLOT_BLOCKS)]
@@ -60,7 +62,7 @@ def tile_xmem_kernel(
         ]
         for g in range(HALVES):
             for b in range(SLOT_BLOCKS):
-                nc.tensor.matmul(dist_ps[g][b][:], mk_sq[:, blocks[b]], sel_neg[:, halves[g]], start=True, stop=False)
+                nc.tensor.matmul(dist_ps[g][b][:], mk_sq[:, b, :], sel_neg[:, halves[g]], start=True, stop=False)
 
         qs = held.tile([CK, N], F32, name="qs")
         qs_x2 = held.tile([CK, N], BF16, name="qs_x2")
@@ -79,7 +81,7 @@ def tile_xmem_kernel(
 
         for g in range(HALVES):
             for b in range(SLOT_BLOCKS):
-                nc.tensor.matmul(dist_ps[g][b][:], mk[:, blocks[b]], qs_x2[:, halves[g]], start=False, stop=False)
+                nc.tensor.matmul(dist_ps[g][b][:], mk_blocks[:, b, :], qs_x2[:, halves[g]], start=False, stop=False)
             for b in range(SLOT_BLOCKS):
                 nc.tensor.matmul(dist_ps[g][b][:], minus_ones[:], qqs_bf[:, halves[g]], start=False, stop=True)
 

@@ -85,27 +85,37 @@ def tile_xmem_kernel(
             for b in range(SLOT_BLOCKS):
                 nc.tensor.matmul(dist_ps[g][b][:], minus_ones[:], qqs_bf[:, halves[g]], start=False, stop=True)
 
-        out_by_block = out.rearrange("(h p) j -> p h j", p=P)
+        expd = [held.tile([P, N], BF16, name=f"expd{b}") for b in range(SLOT_BLOCKS)]
+        inv_sum = held.tile([P, 1, N], F32, name="inv_sum")
         for g in range(HALVES):
-            expd = [held.tile([P, HALF], BF16, name=f"expd{g}_{b}") for b in range(SLOT_BLOCKS)]
-            sum_ps = psum.tile([P, HALF], F32, name=f"sum_ps{g}", tag=f"bank0_{2 * g}")
+            sum_ps = psum.tile([P, HALF], F32, name=f"sum_ps{g}", tag=f"bank0_{g}")
             for b in range(SLOT_BLOCKS):
-                nc.scalar.activation(expd[b][:], dist_ps[g][b][:], FUNC.Exp, scale=exp_scale[:, b : b + 1])
-                nc.tensor.matmul(sum_ps[:], ones[:], expd[b][:], start=(b == 0), stop=(b == SLOT_BLOCKS - 1))
-            inv_sum = held.tile([P, 1, HALF], F32, name=f"inv_sum{g}")
-            nc.vector.reciprocal(inv_sum[:, 0, :], sum_ps[:])
+                nc.scalar.activation(
+                    expd[b][:, halves[g]], dist_ps[g][b][:], FUNC.Exp, scale=exp_scale[:, b : b + 1]
+                )
+                nc.tensor.matmul(
+                    sum_ps[:], ones[:], expd[b][:, halves[g]], start=(b == 0), stop=(b == SLOT_BLOCKS - 1)
+                )
+            nc.vector.reciprocal(inv_sum[:, 0, halves[g]], sum_ps[:])
 
-            read_ps = psum.tile([P, VALUE_BLOCKS, HALF], F32, name=f"read_ps{g}", tag=f"bank0_{2 * g + 1}")
-            for h in range(VALUE_BLOCKS):
-                for b in range(SLOT_BLOCKS):
-                    nc.tensor.matmul(
-                        read_ps[:, h, :],
-                        mv[:, b, h * P : (h + 1) * P],
-                        expd[b][:],
-                        start=(b == 0),
-                        stop=(b == SLOT_BLOCKS - 1),
-                    )
+        mv_by_feature = mv[:].rearrange("p b (f h) -> p b h f", h=VALUE_BLOCKS)
+        read_ps = psum.tile([P, VALUE_BLOCKS, N], F32, name="read_ps", tag="bank0_2")
+        for h in range(VALUE_BLOCKS):
+            for b in range(SLOT_BLOCKS):
+                nc.tensor.matmul(
+                    read_ps[:, h, :],
+                    mv_by_feature[:, b, h, :],
+                    expd[b][:],
+                    start=(b == 0),
+                    stop=(b == SLOT_BLOCKS - 1),
+                )
 
-            read = held.tile([P, VALUE_BLOCKS, HALF], F32, name=f"read{g}")
-            nc.vector.tensor_tensor(read[:], read_ps[:], inv_sum[:].to_broadcast([P, VALUE_BLOCKS, HALF]), ALU.mult)
-            nc.sync.dma_start(out_by_block[:, :, halves[g]], read[:])
+        read = held.tile([P, VALUE_BLOCKS, N], F32, name="read")
+        for g in range(HALVES):
+            nc.vector.tensor_tensor(
+                read[:, :, halves[g]],
+                read_ps[:, :, halves[g]],
+                inv_sum[:, :, halves[g]].to_broadcast([P, VALUE_BLOCKS, HALF]),
+                ALU.mult,
+            )
+        nc.sync.dma_start(out.rearrange("(p h) j -> p h j", h=VALUE_BLOCKS), read[:])

@@ -82,6 +82,7 @@ def tile_xmem_kernel(
         for g in range(HALVES):
             for b in range(SLOT_BLOCKS):
                 nc.tensor.matmul(dist_ps[g][b][:], mk_blocks[:, b, :], qs_x2[:, halves[g]], start=False, stop=False)
+        for g in range(HALVES):
             for b in range(SLOT_BLOCKS):
                 nc.tensor.matmul(dist_ps[g][b][:], minus_ones[:], qqs_bf[:, halves[g]], start=False, stop=True)
 

@@ -46,11 +46,10 @@ def tile_xmem_kernel(
 
         sel_neg = held.tile([CK, N], BF16, name="sel_neg")
         nc.vector.tensor_scalar_mul(sel_neg[:], sel[:], -1.0)
+        mk_sq = held.tile([CK, M], BF16, name="mk_sq")
+        nc.vector.tensor_tensor(mk_sq[:], mk[:], mk[:], ALU.mult)
         mk_by_block = mk[:].rearrange("c (p b) -> c b p", b=SLOT_BLOCKS)
-        mk_sq = held.tile([CK, SLOT_BLOCKS, P], BF16, name="mk_sq")
-        nc.vector.tensor_tensor(mk_sq[:], mk_by_block, mk_by_block, ALU.mult)
-        mk_blocks = held.tile([CK, SLOT_BLOCKS, P], BF16, name="mk_blocks")
-        nc.scalar.copy(mk_blocks[:], mk_by_block)
+        mk_sq_by_block = mk_sq[:].rearrange("c (p b) -> c b p", b=SLOT_BLOCKS)
         exp_scale = held.tile([P, SLOT_BLOCKS], F32, name="exp_scale")
         nc.vector.tensor_scalar_mul(exp_scale[:], shrink[:], 1.0 / math.sqrt(CK))
 
@@ -62,7 +61,7 @@ def tile_xmem_kernel(
         ]
         for g in range(HALVES):
             for b in range(SLOT_BLOCKS):
-                nc.tensor.matmul(dist_ps[g][b][:], mk_sq[:, b, :], sel_neg[:, halves[g]], start=True, stop=False)
+                nc.tensor.matmul(dist_ps[g][b][:], mk_sq_by_block[:, b, :], sel_neg[:, halves[g]], start=True, stop=False)
 
         qs = held.tile([CK, N], F32, name="qs")
         qs_x2 = held.tile([CK, N], BF16, name="qs_x2")
@@ -81,7 +80,7 @@ def tile_xmem_kernel(
 
         for g in range(HALVES):
             for b in range(SLOT_BLOCKS):
-                nc.tensor.matmul(dist_ps[g][b][:], mk_blocks[:, b, :], qs_x2[:, halves[g]], start=False, stop=False)
+                nc.tensor.matmul(dist_ps[g][b][:], mk_by_block[:, b, :], qs_x2[:, halves[g]], start=False, stop=False)
         for g in range(HALVES):
             for b in range(SLOT_BLOCKS):
                 nc.tensor.matmul(dist_ps[g][b][:], minus_ones[:], qqs_bf[:, halves[g]], start=False, stop=True)

@@ -26,12 +26,12 @@ def tile_xmem_kernel(
         tc.tile_pool(name="held", bufs=1) as held,
         tc.psum_pool(name="psum", bufs=1) as psum,
     ):
-        offsets = held.tile([P, N // 16], U16, name="offsets")
-        nc.sync.dma_start(offsets[:], offs)
-        sel = held.tile([CK, N], F32, name="sel")
-        nc.sync.dma_start(sel[:], query_selection)
         mk = held.tile([CK, M], BF16, name="mk")
         nc.sync.dma_start(mk[:], memory_key)
+        sel = held.tile([CK, N], F32, name="sel")
+        nc.sync.dma_start(sel[:], query_selection)
+        offsets = held.tile([P, N // 16], U16, name="offsets")
+        nc.sync.dma_start(offsets[:], offs)
         keys = held.tile([CK, S], F32, name="keys")
         nc.sync.dma_start(keys[:], query_key)
         shrink = held.tile([P, SLOT_BLOCKS], F32, name="shrink")
@@ -39,8 +39,6 @@ def tile_xmem_kernel(
         mv = held.tile([P, SLOT_BLOCKS, V], BF16, name="mv")
         nc.sync.dma_start(mv[:], memory_value.rearrange("(p b) v -> p b v", p=P))
 
-        minus_ones = held.tile([CK, P], BF16, name="minus_ones")
-        nc.vector.memset(minus_ones[:], -1.0)
         ones = held.tile([P, P], BF16, name="ones")
         nc.vector.memset(ones[:], 1.0)
 
@@ -66,7 +64,7 @@ def tile_xmem_kernel(
         qs = held.tile([CK, N], F32, name="qs")
         qs_x2 = held.tile([CK, N], BF16, name="qs_x2")
         qqs = held.tile([CK, N], F32, name="qqs")
-        qqs_bf = held.tile([CK, N], BF16, name="qqs_bf")
+        qqs_neg = held.tile([CK, N], BF16, name="qqs_neg")
         picked = [keys[:].indirect(offsets[:, g * (HALF // 16) : (g + 1) * (HALF // 16)]) for g in range(HALVES)]
         first, second = halves
         nc.vector.tensor_tensor(qs[:, first], picked[0], sel[:, first], ALU.mult)
@@ -74,16 +72,16 @@ def tile_xmem_kernel(
         nc.vector.tensor_scalar_mul(qs_x2[:, first], qs[:, first], 2.0)
         nc.vector.tensor_tensor(qqs[:, first], picked[0], qs[:, first], ALU.mult)
         nc.vector.tensor_scalar_mul(qs_x2[:, second], qs[:, second], 2.0)
-        nc.vector.tensor_copy(qqs_bf[:, first], qqs[:, first])
+        nc.vector.tensor_scalar_mul(qqs_neg[:, first], qqs[:, first], -1.0)
         nc.vector.tensor_tensor(qqs[:, second], picked[1], qs[:, second], ALU.mult)
-        nc.vector.tensor_copy(qqs_bf[:, second], qqs[:, second])
+        nc.vector.tensor_scalar_mul(qqs_neg[:, second], qqs[:, second], -1.0)
 
         for g in range(HALVES):
             for b in range(SLOT_BLOCKS):
                 nc.tensor.matmul(dist_ps[g][b][:], mk_by_block[:, b, :], qs_x2[:, halves[g]], start=False, stop=False)
         for g in range(HALVES):
             for b in range(SLOT_BLOCKS):
-                nc.tensor.matmul(dist_ps[g][b][:], minus_ones[:], qqs_bf[:, halves[g]], start=False, stop=True)
+                nc.tensor.matmul(dist_ps[g][b][:], ones[:], qqs_neg[:, halves[g]], start=False, stop=True)
 
         expd = [held.tile([P, N], BF16, name=f"expd{b}") for b in range(SLOT_BLOCKS)]
         inv_sum = held.tile([P, 1, N], F32, name="inv_sum")

@@ -26,14 +26,14 @@ def tile_xmem_kernel(
         tc.tile_pool(name="held", bufs=1) as held,
         tc.psum_pool(name="psum", bufs=1) as psum,
     ):
+        keys = held.tile([CK, S], F32, name="keys")
+        nc.scalar.dma_start(keys[:], query_key)
         mk = held.tile([CK, M], BF16, name="mk")
         nc.sync.dma_start(mk[:], memory_key)
         sel = held.tile([CK, N], F32, name="sel")
         nc.sync.dma_start(sel[:], query_selection)
         offsets = held.tile([P, N // 16], U16, name="offsets")
         nc.sync.dma_start(offsets[:], offs)
-        keys = held.tile([CK, S], F32, name="keys")
-        nc.sync.dma_start(keys[:], query_key)
         shrink = held.tile([P, SLOT_BLOCKS], F32, name="shrink")
         nc.sync.dma_start(shrink[:], memory_shrinkage.rearrange("(p b) o -> p (b o)", p=P))
         mv = held.tile([P, SLOT_BLOCKS, V], BF16, name="mv")

import math

import concourse.mybir as mybir

F32 = mybir.dt.float32
BF16 = mybir.dt.bfloat16
U16 = mybir.dt.uint16
ALU = mybir.AluOpType
FUNC = mybir.ActivationFunctionType

P = 128
CK, S, N, M, V = 128, 512, 128, 512, 256
SLOT_BLOCKS = M // P
VALUE_BLOCKS = V // P
HALVES = 2
HALF = N // HALVES

FLOPS = 2 * (2 * CK) * M * N + 2 * CK * N + 2 * M * V * N


def tile_xmem_kernel(
    tc, query_key, query_selection, memory_key, memory_shrinkage, memory_value, offs, out
):
    nc = tc.nc
    with (
        tc.tile_pool(name="held", bufs=1) as held,
        tc.psum_pool(name="psum", bufs=1) as psum,
    ):
        keys = held.tile([CK, S], F32, name="keys")
        nc.scalar.dma_start(keys[:], query_key)
        mk = held.tile([CK, M], BF16, name="mk")
        nc.sync.dma_start(mk[:], memory_key)
        sel = held.tile([CK, N], F32, name="sel")
        nc.sync.dma_start(sel[:], query_selection)
        offsets = held.tile([P, N // 16], U16, name="offsets")
        nc.sync.dma_start(offsets[:], offs)
        shrink = held.tile([P, SLOT_BLOCKS], F32, name="shrink")
        nc.sync.dma_start(shrink[:], memory_shrinkage.rearrange("(p b) o -> p (b o)", p=P))
        mv = held.tile([P, SLOT_BLOCKS, V], BF16, name="mv")
        nc.sync.dma_start(mv[:], memory_value.rearrange("(p b) v -> p b v", p=P))

        ones = held.tile([P, P], BF16, name="ones")
        nc.vector.memset(ones[:], 1.0)

        sel_neg = held.tile([CK, N], BF16, name="sel_neg")
        nc.vector.tensor_scalar_mul(sel_neg[:], sel[:], -1.0)
        mk_sq = held.tile([CK, M], BF16, name="mk_sq")
        nc.vector.tensor_tensor(mk_sq[:], mk[:], mk[:], ALU.mult)
        mk_by_block = mk[:].rearrange("c (p b) -> c b p", b=SLOT_BLOCKS)
        mk_sq_by_block = mk_sq[:].rearrange("c (p b) -> c b p", b=SLOT_BLOCKS)
        exp_scale = held.tile([P, SLOT_BLOCKS], F32, name="exp_scale")
        nc.vector.tensor_scalar_mul(exp_scale[:], shrink[:], 1.0 / math.sqrt(CK))

        halves = [slice(g * HALF, (g + 1) * HALF) for g in range(HALVES)]

        dist_ps = [
            [psum.tile([P, HALF], F32, name=f"dist_ps{g}_{b}", tag=f"bank{g}_{b}") for b in range(SLOT_BLOCKS)]
            for g in range(HALVES)
        ]
        for g in range(HALVES):
            for b in range(SLOT_BLOCKS):
                nc.tensor.matmul(dist_ps[g][b][:], mk_sq_by_block[:, b, :], sel_neg[:, halves[g]], start=True, stop=False)

        qs = held.tile([CK, N], F32, name="qs")
        qs_x2 = held.tile([CK, N], BF16, name="qs_x2")
        qqs = held.tile([CK, N], F32, name="qqs")
        qqs_neg = held.tile([CK, N], BF16, name="qqs_neg")
        picked = [keys[:].indirect(offsets[:, g * (HALF // 16) : (g + 1) * (HALF // 16)]) for g in range(HALVES)]
        first, second = halves
        nc.vector.tensor_tensor(qs[:, first], picked[0], sel[:, first], ALU.mult)
        nc.vector.tensor_tensor(qs[:, second], picked[1], sel[:, second], ALU.mult)
        nc.vector.tensor_scalar_mul(qs_x2[:, first], qs[:, first], 2.0)
        nc.vector.tensor_tensor(qqs[:, first], picked[0], qs[:, first], ALU.mult)
        nc.vector.tensor_scalar_mul(qs_x2[:, second], qs[:, second], 2.0)
        nc.vector.tensor_scalar_mul(qqs_neg[:, first], qqs[:, first], -1.0)
        nc.vector.tensor_tensor(qqs[:, second], picked[1], qs[:, second], ALU.mult)
        nc.vector.tensor_scalar_mul(qqs_neg[:, second], qqs[:, second], -1.0)

        for g in range(HALVES):
            for b in range(SLOT_BLOCKS):
                nc.tensor.matmul(dist_ps[g][b][:], mk_by_block[:, b, :], qs_x2[:, halves[g]], start=False, stop=False)
        for g in range(HALVES):
            for b in range(SLOT_BLOCKS):
                nc.tensor.matmul(dist_ps[g][b][:], ones[:], qqs_neg[:, halves[g]], start=False, stop=True)

        expd = [held.tile([P, N], BF16, name=f"expd{b}") for b in range(SLOT_BLOCKS)]
        inv_sum = held.tile([P, 1, N], F32, name="inv_sum")
        for g in range(HALVES):
            sum_ps = psum.tile([P, HALF], F32, name=f"sum_ps{g}", tag=f"bank0_{g}")
            for b in range(SLOT_BLOCKS):
                nc.scalar.activation(
                    expd[b][:, halves[g]], dist_ps[g][b][:], FUNC.Exp, scale=exp_scale[:, b : b + 1]
                )
                nc.tensor.matmul(
                    sum_ps[:], ones[:], expd[b][:, halves[g]], start=(b == 0), stop=(b == SLOT_BLOCKS - 1)
                )
            nc.vector.reciprocal(inv_sum[:, 0, halves[g]], sum_ps[:])

        mv_by_feature = mv[:].rearrange("p b (f h) -> p b h f", h=VALUE_BLOCKS)
        read_ps = psum.tile([P, VALUE_BLOCKS, N], F32, name="read_ps", tag="bank0_2")
        for h in range(VALUE_BLOCKS):
            for b in range(SLOT_BLOCKS):
                nc.tensor.matmul(
                    read_ps[:, h, :],
                    mv_by_feature[:, b, h, :],
                    expd[b][:],
                    start=(b == 0),
                    stop=(b == SLOT_BLOCKS - 1),
                )

        read = held.tile([P, VALUE_BLOCKS, N], F32, name="read")
        for g in range(HALVES):
            nc.vector.tensor_tensor(
                read[:, :, halves[g]],
                read_ps[:, :, halves[g]],
                inv_sum[:, :, halves[g]].to_broadcast([P, VALUE_BLOCKS, HALF]),
                ALU.mult,
            )
        nc.sync.dma_start(out.rearrange("(p h) j -> p h j", h=VALUE_BLOCKS), read[:])
